import numpy as np
import ml_dtypes


def mxq(x, axis, fmt="e4m3"):
    dtype, down = {"e4m3": (ml_dtypes.float8_e4m3fn, 7), "e5m2": (ml_dtypes.float8_e5m2, 14)}[fmt]
    v = np.moveaxis(np.asarray(x, np.float32).astype(ml_dtypes.bfloat16).astype(np.float64), axis, -1)
    blocks = v.reshape(v.shape[:-1] + (-1, 32))
    amax = np.abs(blocks).max(-1, keepdims=True)
    byte = np.maximum(np.where(amax > 0, np.frexp(amax)[1] - 1 + 127, 0) - down, 1)
    scale = np.exp2(byte - 127.0)
    codes = (blocks / scale).astype(np.float32).astype(dtype).astype(np.float64)
    return np.moveaxis((codes * scale).reshape(v.shape), -1, axis)


WIDE = False


def mx_kscale(k):
    if not WIDE:
        return np.ones(k)
    levels = np.array([10, -10, 5, -5, 0])
    a = np.random.permutation(np.resize(levels, k // 512 * 4)).reshape(k // 512, 4)
    idx = np.arange(k)
    return np.exp2(a[idx // 512, idx % 128 // 32])


BF16 = ml_dtypes.bfloat16


def bf(x):
    return np.asarray(x, np.float32).astype(BF16)


def f64(x):
    return np.asarray(x).astype(np.float64)


B, K, N = 4096, 512, 1024


def setup_inputs():
    s = mx_kscale(K)
    c = s[:, None]
    return {
        "input": bf(np.random.standard_normal((B, N)) * 0.5),
        "yin": bf(np.random.standard_normal((B, K)) * s),
        "hebb": bf(np.random.standard_normal((K, N)) * c),
        "w": bf(np.random.standard_normal((K, N)) * 0.5 / np.sqrt(K) / c),
        "alpha": bf(np.random.standard_normal((K, N)) * 0.5 / np.sqrt(K) / (c * c)),
        "eta": bf(np.random.uniform(0.2, 0.4, 1)),
    }


def reference(input, yin, hebb, w, alpha, eta):
    yin, hebb, eta = f64(yin), f64(hebb), f64(eta)
    weff = f64(w) + f64(alpha) * hebb
    yout = np.tanh((mxq(yin, 1, "e4m3") @ mxq(weff, 0, "e4m3")) + f64(input))
    hebb_new = (1.0 - eta) * hebb + eta * (yin[0][:, None] * yout[0][None, :])
    return yout, hebb_new

@@ -1,0 +1,209 @@
+from contextlib import ExitStack
+
+import concourse.mybir as mybir
+from concourse.masks import make_identity
+
+F32 = mybir.dt.float32
+BF16 = mybir.dt.bfloat16
+U32 = mybir.dt.uint32
+U8 = mybir.dt.uint8
+FP8X4 = mybir.dt.float8_e4m3fn_x4
+ADD = mybir.AluOpType.add
+MULT = mybir.AluOpType.mult
+ACT = mybir.ActivationFunctionType
+
+P = 128
+B, K, N = 4096, 512, 1024
+NT = B // P
+HALF = 512
+GROUP = 4
+NG = NT // GROUP
+FLOPS = 2 * B * K * N
+
+
+def tile_plasticlayer_t_kernel(tc, inp, yin, hebb, w, alpha, eta, out_0, out_1):
+    nc = tc.nc
+    with ExitStack() as ctx:
+        const = ctx.enter_context(tc.tile_pool(name="const", bufs=1))
+        wpool = ctx.enter_context(tc.tile_pool(name="wpool", bufs=1))
+        ypool = ctx.enter_context(tc.tile_pool(name="ypool", bufs=1))
+        ipool = ctx.enter_context(tc.tile_pool(name="ipool", bufs=1))
+        gpool = ctx.enter_context(tc.tile_pool(name="gpool", bufs=3))
+        spool = ctx.enter_context(tc.tile_pool(name="spool", bufs=6))
+        xpool = ctx.enter_context(tc.psum_pool(name="xpool", bufs=2))
+        apool = ctx.enter_context(tc.psum_pool(name="apool", bufs=6))
+        ctx.enter_context(tc.manual_schedule())
+
+        yin_v = yin.rearrange("(p t) k -> p (t k)", t=NT)
+        inp_v = inp.rearrange("(p t) n -> p (t n)", t=NT)
+        out_v = out_0.rearrange("(p t) n -> p (t n)", t=NT)
+
+        def k_half(x, u):
+            return x[256 * u : 256 * (u + 1), :].rearrange("(p e) n -> p (e n)", e=2)
+
+        eta_bf = const.tile([P, 1], BF16, name="eta_bf")
+        nc.scalar.dma_start(out=eta_bf[:], in_=eta.partition_broadcast(P))
+
+        wt = {}
+        for u in range(2):
+            for nm, src in (("alpha", alpha), ("hebb", hebb), ("w", w)):
+                t_ = wpool.tile([P, 2 * N], BF16, name="%s%d" % (nm, u))
+                nc.sync.dma_start(out=t_[:], in_=k_half(src, u))
+                wt[(nm, u)] = t_
+
+        ychunk = []
+        iloc = {}
+
+        def load_y(c):
+            t_ = ypool.tile([P, 8 * K], BF16, name="y%d" % c)
+            nc.sync.dma_start(out=t_[:], in_=yin_v[:, 8 * c * K : 8 * (c + 1) * K])
+            ychunk.append(t_)
+
+        def load_i(t0, n_tiles):
+            t_ = ipool.tile([P, n_tiles * N], BF16, name="i%d" % t0)
+            nc.sync.dma_start(out=t_[:], in_=inp_v[:, t0 * N : (t0 + n_tiles) * N])
+            for j in range(n_tiles):
+                iloc[t0 + j] = (t_, j * N)
+
+        load_y(0)
+        load_i(0, 4)
+        load_i(4, 4)
+        for c in range(1, 4):
+            load_y(c)
+            load_i(8 * c, 8)
+
+        warm = const.tile([P, 1], F32, name="warm")
+        warm2 = const.tile([P, 1], F32, name="warm2")
+        nc.vector.memset(warm[:], 0.0)
+        nc.scalar.activation(out=warm2[:], in_=warm[:], func=ACT.Tanh)
+        ident = const.tile([P, P], F32, name="ident")
+        make_identity(nc, ident[:])
+        eta_f = const.tile([P, 1], F32, name="eta_f")
+        om = const.tile([P, 1], F32, name="om")
+        nc.vector.tensor_copy(out=eta_f[:], in_=eta_bf[:])
+        nc.vector.tensor_scalar(out=om[:], in0=eta_bf[:], scalar1=-1.0, scalar2=1.0, op0=MULT, op1=ADD)
+
+        wg = wpool.tile([P, 4 * N], BF16, name="wg", align_bytes=64)
+        wg_v = wg[:].rearrange("p (n u e) -> p u n e", u=2, e=2)
+        wcodes = wpool.tile([P, N], U32, name="wcodes", align_bytes=64)
+        wscales = wpool.tile([P, N], U8, name="wscales", align_bytes=64)
+        hn = []
+        for u in range(2):
+            tmp = wpool.tile([P, 2 * N], F32, name="tmp%d" % u)
+            nc.vector.tensor_tensor(out=tmp[:], in0=wt[("alpha", u)][:], in1=wt[("hebb", u)][:], op=MULT)
+            nc.vector.tensor_tensor(
+                out=wg_v[:, u],
+                in0=tmp[:].rearrange("p (e n) -> p n e", e=2),
+                in1=wt[("w", u)][:].rearrange("p (e n) -> p n e", e=2),
+                op=ADD,
+            )
+            hn_u = wpool.tile([P, 2 * N], F32, name="hn%d" % u)
+            nc.scalar.activation(out=hn_u[:], in_=wt[("hebb", u)][:], func=ACT.Copy, scale=om[:, 0:1])
+            hn.append(hn_u)
+
+        def transposes(g):
+            banks = []
+            for j in range(2):
+                xt = xpool.tile([P, HALF], F32, name="xt")
+                for i in range(2):
+                    t = GROUP * g + 2 * j + i
+                    yw = ychunk[t // 8][:].bitcast(F32)
+                    for u in range(2):
+                        c0 = (t % 8) * 256 + u * P
+                        s0 = (2 * i + u) * P
+                        nc.tensor.transpose(xt[:, s0 : s0 + P], yw[:, c0 : c0 + P], ident[:])
+                banks.append(xt)
+            return banks
+
+        def regroup(banks):
+            grouped = gpool.tile([P, GROUP * K], BF16, name="grouped", align_bytes=64, bufs=2)
+            gw = grouped[:].bitcast(F32)
+            for j in range(2):
+                nc.scalar.copy(
+                    out=gw[:, j * HALF : (j + 1) * HALF].rearrange("p (i b u) -> p i b u", i=2, u=2),
+                    in_=banks[j][:].rearrange("p (i u b) -> p i b u", i=2, u=2),
+                )
+            return grouped
+
+        def quantise(grouped):
+            ycodes = gpool.tile([P, GROUP * P], U32, name="ycodes", align_bytes=64)
+            yscales = gpool.tile([P, GROUP * P], U8, name="yscales", align_bytes=64)
+            nc.vector.quantize_mx(out=ycodes[:].bitcast(FP8X4), scales=yscales[:], in_=grouped[:])
+            return ycodes, yscales
+
+        banks = transposes(0)
+        grouped = regroup(banks)
+        q_next = quantise(grouped)
+        s_k = const.tile([P, 4], F32, name="s_k")
+        nc.vector.tensor_scalar(out=s_k[:], in0=grouped[:, 0:4], scalar1=eta_f[:, 0:1], scalar2=None, op0=MULT)
+        for h in range(2):
+            nc.vector.quantize_mx(
+                out=wcodes[:, h * HALF : (h + 1) * HALF].bitcast(FP8X4),
+                scales=wscales[:, h * HALF : (h + 1) * HALF],
+                in_=wg[:, h * 4 * HALF : (h + 1) * 4 * HALF],
+            )
+        banks = transposes(1)
+
+        st0 = None
+        yb = []
+        for g in range(NG):
+            ycodes, yscales = q_next
+            if g + 1 < NG:
+                grouped = regroup(banks)
+            st = None
+            for i in range(GROUP):
+                t = GROUP * g + i
+                if i % 2 == 0:
+                    st = spool.tile([P, 2 * N], F32, name="st")
+                    if t == 0:
+                        st0 = st
+                base = (i % 2) * N
+                itile, ioff = iloc[t]
+                for h in range(2):
+                    acc = apool.tile([P, HALF], F32, name="acc")
+                    nc.tensor.matmul_mx(
+                        out=acc[:],
+                        lhsT=ycodes[:, i * P : (i + 1) * P].bitcast(FP8X4),
+                        lhsT_scale=yscales[:, i * P : (i + 1) * P],
+                        rhs=wcodes[:, h * HALF : (h + 1) * HALF].bitcast(FP8X4),
+                        rhs_scale=wscales[:, h * HALF : (h + 1) * HALF],
+                        start=True,
+                        stop=True,
+                    )
+                    nc.vector.tensor_tensor(
+                        out=st[:, base + h * HALF : base + (h + 1) * HALF],
+                        in0=acc[:],
+                        in1=itile[:, ioff + h * HALF : ioff + (h + 1) * HALF],
+                        op=ADD,
+                    )
+                nc.scalar.activation(out=st[:, base : base + N], in_=st[:, base : base + N], func=ACT.Tanh)
+                if g == 1:
+                    for h in range(2):
+                        c0 = (i % 2) * N + h * HALF
+                        nc.vector.scalar_tensor_tensor(
+                            out=hn[i // 2][:, c0 : c0 + HALF],
+                            in0=yb[h][:],
+                            scalar=s_k[:, i : i + 1],
+                            in1=hn[i // 2][:, c0 : c0 + HALF],
+                            op0=MULT,
+                            op1=ADD,
+                        )
+                if i % 2 == 1:
+                    nc.sync.dma_start(out=out_v[:, (t - 1) * N : (t + 1) * N], in_=st[:])
+                    if g == 1:
+                        nc.sync.dma_start(out=k_half(out_1, i // 2), in_=hn[i // 2][:])
+                if i == 1 and g + 1 < NG:
+                    q_next = quantise(grouped)
+            if g + 2 < NG:
+                banks = transposes(g + 2)
+            if g == 0:
+                for h in range(2):
+                    yb_h = apool.tile([P, HALF], F32, name="yb%d" % h, tag="acc")
+                    nc.tensor.matmul(
+                        out=yb_h[:],
+                        lhsT=ident[:, 0:1].to_broadcast([P, P]),
+                        rhs=st0[:, h * HALF : (h + 1) * HALF],
+                        start=True,
+                        stop=True,
+                    )
+                    yb.append(yb_h)

@@ -29,7 +29,7 @@ def tile_plasticlayer_t_kernel(tc, inp, yin, hebb, w, alpha, eta, out_0, out_1):
         ypool = ctx.enter_context(tc.tile_pool(name="ypool", bufs=1))
         ipool = ctx.enter_context(tc.tile_pool(name="ipool", bufs=1))
         gpool = ctx.enter_context(tc.tile_pool(name="gpool", bufs=3))
-        spool = ctx.enter_context(tc.tile_pool(name="spool", bufs=6))
+        spool = ctx.enter_context(tc.tile_pool(name="spool", bufs=4))
         xpool = ctx.enter_context(tc.psum_pool(name="xpool", bufs=2))
         apool = ctx.enter_context(tc.psum_pool(name="apool", bufs=6))
         ctx.enter_context(tc.manual_schedule())
@@ -41,8 +41,12 @@ def tile_plasticlayer_t_kernel(tc, inp, yin, hebb, w, alpha, eta, out_0, out_1):
         def k_half(x, u):
             return x[256 * u : 256 * (u + 1), :].rearrange("(p e) n -> p (e n)", e=2)
 
-        eta_bf = const.tile([P, 1], BF16, name="eta_bf")
-        nc.scalar.dma_start(out=eta_bf[:], in_=eta.partition_broadcast(P))
+        sel = const.tile([P, P], BF16, name="sel")
+        nc.vector.memset(sel[:], 0.0)
+        nc.vector.memset(sel[0:1, :], 1.0)
+        eta_row = const.tile([P, 32], BF16, name="eta_row")
+        nc.vector.memset(eta_row[:], 0.0)
+        nc.scalar.dma_start(out=eta_row[0:1, 0:1], in_=eta.rearrange("(o x) -> o x", o=1))
 
         wt = {}
         for u in range(2):
@@ -67,8 +71,10 @@ def tile_plasticlayer_t_kernel(tc, inp, yin, hebb, w, alpha, eta, out_0, out_1):
 
         load_y(0)
         load_i(0, 4)
+        load_y(1)
         load_i(4, 4)
-        for c in range(1, 4):
+        load_i(8, 8)
+        for c in range(2, 4):
             load_y(c)
             load_i(8 * c, 8)
 
@@ -80,20 +86,24 @@ def tile_plasticlayer_t_kernel(tc, inp, yin, hebb, w, alpha, eta, out_0, out_1):
         make_identity(nc, ident[:])
         eta_f = const.tile([P, 1], F32, name="eta_f")
         om = const.tile([P, 1], F32, name="om")
-        nc.vector.tensor_copy(out=eta_f[:], in_=eta_bf[:])
-        nc.vector.tensor_scalar(out=om[:], in0=eta_bf[:], scalar1=-1.0, scalar2=1.0, op0=MULT, op1=ADD)
+        eta_ps = apool.tile([P, HALF], F32, name="eta_ps", tag="acc")
+        nc.tensor.matmul(out=eta_ps[:, 0:32], lhsT=sel[:], rhs=eta_row[:], start=True, stop=True)
 
         wg = wpool.tile([P, 4 * N], BF16, name="wg", align_bytes=64)
         wg_v = wg[:].rearrange("p (n u e) -> p u n e", u=2, e=2)
         wcodes = wpool.tile([P, N], U32, name="wcodes", align_bytes=64)
         wscales = wpool.tile([P, N], U8, name="wscales", align_bytes=64)
         hn = []
+        tmp_all = spool.tile([P, 4 * N], F32, name="tmp_all", tag="st")
         for u in range(2):
-            tmp = wpool.tile([P, 2 * N], F32, name="tmp%d" % u)
-            nc.vector.tensor_tensor(out=tmp[:], in0=wt[("alpha", u)][:], in1=wt[("hebb", u)][:], op=MULT)
+            tmp = tmp_all[:, u * 2 * N : (u + 1) * 2 * N]
+            nc.vector.tensor_tensor(out=tmp, in0=wt[("alpha", u)][:], in1=wt[("hebb", u)][:], op=MULT)
+            if u == 0:
+                nc.vector.tensor_copy(out=eta_f[:], in_=eta_ps[:, 0:1])
+                nc.vector.tensor_scalar(out=om[:], in0=eta_ps[:, 0:1], scalar1=-1.0, scalar2=1.0, op0=MULT, op1=ADD)
             nc.vector.tensor_tensor(
                 out=wg_v[:, u],
-                in0=tmp[:].rearrange("p (e n) -> p n e", e=2),
+                in0=tmp.rearrange("p (e n) -> p n e", e=2),
                 in1=wt[("w", u)][:].rearrange("p (e n) -> p n e", e=2),
                 op=ADD,
             )
@@ -143,67 +153,72 @@ def tile_plasticlayer_t_kernel(tc, inp, yin, hebb, w, alpha, eta, out_0, out_1):
                 in_=wg[:, h * 4 * HALF : (h + 1) * 4 * HALF],
             )
         banks = transposes(1)
+        grouped = regroup(banks)
 
+        st = None
         st0 = None
         yb = []
-        for g in range(NG):
-            ycodes, yscales = q_next
-            if g + 1 < NG:
-                grouped = regroup(banks)
-            st = None
-            for i in range(GROUP):
-                t = GROUP * g + i
-                if i % 2 == 0:
-                    st = spool.tile([P, 2 * N], F32, name="st")
-                    if t == 0:
-                        st0 = st
-                base = (i % 2) * N
-                itile, ioff = iloc[t]
-                for h in range(2):
-                    acc = apool.tile([P, HALF], F32, name="acc")
-                    nc.tensor.matmul_mx(
-                        out=acc[:],
-                        lhsT=ycodes[:, i * P : (i + 1) * P].bitcast(FP8X4),
-                        lhsT_scale=yscales[:, i * P : (i + 1) * P],
-                        rhs=wcodes[:, h * HALF : (h + 1) * HALF].bitcast(FP8X4),
-                        rhs_scale=wscales[:, h * HALF : (h + 1) * HALF],
-                        start=True,
-                        stop=True,
-                    )
-                    nc.vector.tensor_tensor(
-                        out=st[:, base + h * HALF : base + (h + 1) * HALF],
-                        in0=acc[:],
-                        in1=itile[:, ioff + h * HALF : ioff + (h + 1) * HALF],
-                        op=ADD,
-                    )
-                nc.scalar.activation(out=st[:, base : base + N], in_=st[:, base : base + N], func=ACT.Tanh)
-                if g == 1:
-                    for h in range(2):
-                        c0 = (i % 2) * N + h * HALF
-                        nc.vector.scalar_tensor_tensor(
-                            out=hn[i // 2][:, c0 : c0 + HALF],
-                            in0=yb[h][:],
-                            scalar=s_k[:, i : i + 1],
-                            in1=hn[i // 2][:, c0 : c0 + HALF],
-                            op0=MULT,
-                            op1=ADD,
-                        )
-                if i % 2 == 1:
-                    nc.sync.dma_start(out=out_v[:, (t - 1) * N : (t + 1) * N], in_=st[:])
-                    if g == 1:
-                        nc.sync.dma_start(out=k_half(out_1, i // 2), in_=hn[i // 2][:])
-                if i == 1 and g + 1 < NG:
-                    q_next = quantise(grouped)
-            if g + 2 < NG:
+        ycodes, yscales = q_next
+        for t in range(NT):
+            g, i = divmod(t, GROUP)
+            if i == 0:
+                ycodes, yscales = q_next
+                st = spool.tile([P, GROUP * N], F32, name="st")
+                if g == 0:
+                    st0 = st
+            base = i * N
+            itile, ioff = iloc[t]
+            for h in range(2):
+                acc = apool.tile([P, HALF], F32, name="acc")
+                nc.tensor.matmul_mx(
+                    out=acc[:],
+                    lhsT=ycodes[:, i * P : (i + 1) * P].bitcast(FP8X4),
+                    lhsT_scale=yscales[:, i * P : (i + 1) * P],
+                    rhs=wcodes[:, h * HALF : (h + 1) * HALF].bitcast(FP8X4),
+                    rhs_scale=wscales[:, h * HALF : (h + 1) * HALF],
+                    start=True,
+                    stop=True,
+                )
+                nc.vector.tensor_tensor(
+                    out=st[:, base + h * HALF : base + (h + 1) * HALF],
+                    in0=acc[:],
+                    in1=itile[:, ioff + h * HALF : ioff + (h + 1) * HALF],
+                    op=ADD,
+                )
+            if i == 0 and g + 1 < NG:
+                q_next = quantise(grouped)
+            if i == 1 and g + 2 < NG:
                 banks = transposes(g + 2)
-            if g == 0:
+            if i == 2 and g + 2 < NG:
+                grouped = regroup(banks)
+            nc.scalar.activation(out=st[:, base : base + N], in_=st[:, base : base + N], func=ACT.Tanh)
+            if t in (3, 4):
+                h = t - 3
+                yb_h = apool.tile([P, HALF], F32, name="yb%d" % h, tag="acc")
+                nc.tensor.matmul(
+                    out=yb_h[:],
+                    lhsT=ident[:, 0:1].to_broadcast([P, P]),
+                    rhs=st0[:, h * HALF : (h + 1) * HALF],
+                    start=True,
+                    stop=True,
+                )
+                yb.append(yb_h)
+            if 5 <= t < 9:
+                j = t - 5
                 for h in range(2):
-                    yb_h = apool.tile([P, HALF], F32, name="yb%d" % h, tag="acc")
-                    nc.tensor.matmul(
-                        out=yb_h[:],
-                        lhsT=ident[:, 0:1].to_broadcast([P, P]),
-                        rhs=st0[:, h * HALF : (h + 1) * HALF],
-                        start=True,
-                        stop=True,
+                    c0 = (j % 2) * N + h * HALF
+                    nc.vector.scalar_tensor_tensor(
+                        out=hn[j // 2][:, c0 : c0 + HALF],
+                        in0=yb[h][:],
+                        scalar=s_k[:, j : j + 1],
+                        in1=hn[j // 2][:, c0 : c0 + HALF],
+                        op0=MULT,
+                        op1=ADD,
                     )
-                    yb.append(yb_h)
+                if j % 2 == 1:
+                    nc.sync.dma_start(out=k_half(out_1, j // 2), in_=hn[j // 2][:])
+            if g < NG - 1:
+                if i == GROUP - 1:
+                    nc.sync.dma_start(out=out_v[:, (t - 3) * N : (t + 1) * N], in_=st[:])
+            elif i % 2 == 1:
+                nc.sync.dma_start(out=out_v[:, (t - 1) * N : (t + 1) * N], in_=st[:, (i - 1) * N : (i + 1) * N])

@@ -38,8 +38,8 @@ def tile_plasticlayer_t_kernel(tc, inp, yin, hebb, w, alpha, eta, out_0, out_1):
         inp_v = inp.rearrange("(p t) n -> p (t n)", t=NT)
         out_v = out_0.rearrange("(p t) n -> p (t n)", t=NT)
 
-        def k_half(x, u):
-            return x[256 * u : 256 * (u + 1), :].rearrange("(p e) n -> p (e n)", e=2)
+        def k_rows(x):
+            return x.rearrange("(p j) n -> p (j n)", j=4)
 
         sel = const.tile([P, P], BF16, name="sel")
         nc.vector.memset(sel[:], 0.0)
@@ -49,19 +49,19 @@ def tile_plasticlayer_t_kernel(tc, inp, yin, hebb, w, alpha, eta, out_0, out_1):
         nc.scalar.dma_start(out=eta_row[0:1, 0:1], in_=eta.rearrange("(o x) -> o x", o=1))
 
         wt = {}
-        for u in range(2):
-            for nm, src in (("alpha", alpha), ("hebb", hebb), ("w", w)):
-                t_ = wpool.tile([P, 2 * N], BF16, name="%s%d" % (nm, u))
-                nc.sync.dma_start(out=t_[:], in_=k_half(src, u))
-                wt[(nm, u)] = t_
+        for nm, src in (("alpha", alpha), ("hebb", hebb), ("w", w)):
+            t_ = wpool.tile([P, 4 * N], BF16, name=nm)
+            nc.sync.dma_start(out=t_[:], in_=k_rows(src))
+            wt[nm] = t_
 
-        ychunk = []
+        yloc = {}
         iloc = {}
 
-        def load_y(c):
-            t_ = ypool.tile([P, 8 * K], BF16, name="y%d" % c)
-            nc.sync.dma_start(out=t_[:], in_=yin_v[:, 8 * c * K : 8 * (c + 1) * K])
-            ychunk.append(t_)
+        def load_y(t0, n_tiles):
+            t_ = ypool.tile([P, n_tiles * K], BF16, name="y%d" % t0)
+            nc.sync.dma_start(out=t_[:], in_=yin_v[:, t0 * K : (t0 + n_tiles) * K])
+            for j in range(n_tiles):
+                yloc[t0 + j] = (t_, j * (K // 2))
 
         def load_i(t0, n_tiles):
             t_ = ipool.tile([P, n_tiles * N], BF16, name="i%d" % t0)
@@ -69,14 +69,13 @@ def tile_plasticlayer_t_kernel(tc, inp, yin, hebb, w, alpha, eta, out_0, out_1):
             for j in range(n_tiles):
                 iloc[t0 + j] = (t_, j * N)
 
-        load_y(0)
+        load_y(0, 8)
         load_i(0, 4)
-        load_y(1)
+        load_y(8, 8)
         load_i(4, 4)
         load_i(8, 8)
-        for c in range(2, 4):
-            load_y(c)
-            load_i(8 * c, 8)
+        load_y(16, 16)
+        load_i(16, 16)
 
         warm = const.tile([P, 1], F32, name="warm")
         warm2 = const.tile([P, 1], F32, name="warm2")
@@ -93,23 +92,20 @@ def tile_plasticlayer_t_kernel(tc, inp, yin, hebb, w, alpha, eta, out_0, out_1):
         wg_v = wg[:].rearrange("p (n u e) -> p u n e", u=2, e=2)
         wcodes = wpool.tile([P, N], U32, name="wcodes", align_bytes=64)
         wscales = wpool.tile([P, N], U8, name="wscales", align_bytes=64)
-        hn = []
+        nc.vector.tensor_copy(out=eta_f[:], in_=eta_ps[:, 0:1])
+        nc.vector.tensor_scalar(out=om[:], in0=eta_ps[:, 0:1], scalar1=-1.0, scalar2=1.0, op0=MULT, op1=ADD)
+        hn = wpool.tile([P, 4 * N], F32, name="hn")
+        nc.scalar.activation(out=hn[:], in_=wt["hebb"][:], func=ACT.Copy, scale=om[:, 0:1])
         tmp_all = spool.tile([P, 4 * N], F32, name="tmp_all", tag="st")
+        nc.vector.tensor_tensor(out=tmp_all[:], in0=wt["alpha"][:], in1=wt["hebb"][:], op=MULT)
         for u in range(2):
-            tmp = tmp_all[:, u * 2 * N : (u + 1) * 2 * N]
-            nc.vector.tensor_tensor(out=tmp, in0=wt[("alpha", u)][:], in1=wt[("hebb", u)][:], op=MULT)
-            if u == 0:
-                nc.vector.tensor_copy(out=eta_f[:], in_=eta_ps[:, 0:1])
-                nc.vector.tensor_scalar(out=om[:], in0=eta_ps[:, 0:1], scalar1=-1.0, scalar2=1.0, op0=MULT, op1=ADD)
+            cols = slice(u * 2 * N, (u + 1) * 2 * N)
             nc.vector.tensor_tensor(
                 out=wg_v[:, u],
-                in0=tmp.rearrange("p (e n) -> p n e", e=2),
-                in1=wt[("w", u)][:].rearrange("p (e n) -> p n e", e=2),
+                in0=tmp_all[:, cols].rearrange("p (e n) -> p n e", e=2),
+                in1=wt["w"][:, cols].rearrange("p (e n) -> p n e", e=2),
                 op=ADD,
             )
-            hn_u = wpool.tile([P, 2 * N], F32, name="hn%d" % u)
-            nc.scalar.activation(out=hn_u[:], in_=wt[("hebb", u)][:], func=ACT.Copy, scale=om[:, 0:1])
-            hn.append(hn_u)
 
         def transposes(g):
             banks = []
@@ -117,11 +113,11 @@ def tile_plasticlayer_t_kernel(tc, inp, yin, hebb, w, alpha, eta, out_0, out_1):
                 xt = xpool.tile([P, HALF], F32, name="xt")
                 for i in range(2):
                     t = GROUP * g + 2 * j + i
-                    yw = ychunk[t // 8][:].bitcast(F32)
+                    ytile, c0 = yloc[t]
+                    yw = ytile[:].bitcast(F32)
                     for u in range(2):
-                        c0 = (t % 8) * 256 + u * P
                         s0 = (2 * i + u) * P
-                        nc.tensor.transpose(xt[:, s0 : s0 + P], yw[:, c0 : c0 + P], ident[:])
+                        nc.tensor.transpose(xt[:, s0 : s0 + P], yw[:, c0 + u : c0 + K // 2 : 2], ident[:])
                 banks.append(xt)
             return banks
 
@@ -206,17 +202,17 @@ def tile_plasticlayer_t_kernel(tc, inp, yin, hebb, w, alpha, eta, out_0, out_1):
             if 5 <= t < 9:
                 j = t - 5
                 for h in range(2):
-                    c0 = (j % 2) * N + h * HALF
+                    c0 = j * N + h * HALF
                     nc.vector.scalar_tensor_tensor(
-                        out=hn[j // 2][:, c0 : c0 + HALF],
+                        out=hn[:, c0 : c0 + HALF],
                         in0=yb[h][:],
                         scalar=s_k[:, j : j + 1],
-                        in1=hn[j // 2][:, c0 : c0 + HALF],
+                        in1=hn[:, c0 : c0 + HALF],
                         op0=MULT,
                         op1=ADD,
                     )
-                if j % 2 == 1:
-                    nc.sync.dma_start(out=k_half(out_1, j // 2), in_=hn[j // 2][:])
+                if j == 3:
+                    nc.sync.dma_start(out=k_rows(out_1), in_=hn[:])
             if g < NG - 1:
                 if i == GROUP - 1:
                     nc.sync.dma_start(out=out_v[:, (t - 3) * N : (t + 1) * N], in_=st[:])

@@ -41,18 +41,19 @@ def tile_plasticlayer_t_kernel(tc, inp, yin, hebb, w, alpha, eta, out_0, out_1):
         def k_rows(x):
             return x.rearrange("(p j) n -> p (j n)", j=4)
 
+        eta_row = const.tile([P, 32], BF16, name="eta_row")
+        nc.vector.memset(eta_row[:], 0.0)
         sel = const.tile([P, P], BF16, name="sel")
         nc.vector.memset(sel[:], 0.0)
         nc.vector.memset(sel[0:1, :], 1.0)
-        eta_row = const.tile([P, 32], BF16, name="eta_row")
-        nc.vector.memset(eta_row[:], 0.0)
-        nc.scalar.dma_start(out=eta_row[0:1, 0:1], in_=eta.rearrange("(o x) -> o x", o=1))
 
         wt = {}
         for nm, src in (("alpha", alpha), ("hebb", hebb), ("w", w)):
             t_ = wpool.tile([P, 4 * N], BF16, name=nm)
             nc.sync.dma_start(out=t_[:], in_=k_rows(src))
             wt[nm] = t_
+            if nm == "alpha":
+                nc.sync.dma_start(out=eta_row[0:1, 0:1], in_=eta.rearrange("(o x) -> o x", o=1))
 
         yloc = {}
         iloc = {}
@@ -70,9 +71,8 @@ def tile_plasticlayer_t_kernel(tc, inp, yin, hebb, w, alpha, eta, out_0, out_1):
                 iloc[t0 + j] = (t_, j * N)
 
         load_y(0, 8)
-        load_i(0, 4)
+        load_i(0, 8)
         load_y(8, 8)
-        load_i(4, 4)
         load_i(8, 8)
         load_y(16, 16)
         load_i(16, 16)
@@ -92,8 +92,8 @@ def tile_plasticlayer_t_kernel(tc, inp, yin, hebb, w, alpha, eta, out_0, out_1):
         wg_v = wg[:].rearrange("p (n u e) -> p u n e", u=2, e=2)
         wcodes = wpool.tile([P, N], U32, name="wcodes", align_bytes=64)
         wscales = wpool.tile([P, N], U8, name="wscales", align_bytes=64)
-        nc.vector.tensor_copy(out=eta_f[:], in_=eta_ps[:, 0:1])
-        nc.vector.tensor_scalar(out=om[:], in0=eta_ps[:, 0:1], scalar1=-1.0, scalar2=1.0, op0=MULT, op1=ADD)
+        nc.scalar.copy(out=eta_f[:], in_=eta_ps[:, 0:1])
+        nc.scalar.activation(out=om[:], in_=eta_ps[:, 0:1], func=ACT.Copy, bias=1.0, scale=-1.0)
         hn = wpool.tile([P, 4 * N], F32, name="hn")
         nc.scalar.activation(out=hn[:], in_=wt["hebb"][:], func=ACT.Copy, scale=om[:, 0:1])
         tmp_all = spool.tile([P, 4 * N], F32, name="tmp_all", tag="st")

@@ -153,7 +153,7 @@ def tile_plasticlayer_t_kernel(tc, inp, yin, hebb, w, alpha, eta, out_0, out_1):
 
         st = None
         st0 = None
-        yb = []
+        ybs = wpool.tile([P, N], F32, name="ybs")
         ycodes, yscales = q_next
         for t in range(NT):
             g, i = divmod(t, GROUP)
@@ -198,21 +198,21 @@ def tile_plasticlayer_t_kernel(tc, inp, yin, hebb, w, alpha, eta, out_0, out_1):
                     start=True,
                     stop=True,
                 )
-                yb.append(yb_h)
-            if 5 <= t < 9:
-                j = t - 5
-                for h in range(2):
+                nc.scalar.copy(out=ybs[:, h * HALF : (h + 1) * HALF], in_=yb_h[:])
+                for j in range(4):
                     c0 = j * N + h * HALF
-                    nc.vector.scalar_tensor_tensor(
-                        out=hn[:, c0 : c0 + HALF],
-                        in0=yb[h][:],
-                        scalar=s_k[:, j : j + 1],
-                        in1=hn[:, c0 : c0 + HALF],
+                    outer = gpool.tile([P, HALF], F32, name="outer", bufs=2)
+                    nc.gpsimd.tensor_scalar(
+                        out=outer[:],
+                        in0=ybs[:, h * HALF : (h + 1) * HALF],
+                        scalar1=s_k[:, j : j + 1],
+                        scalar2=0.0,
                         op0=MULT,
                         op1=ADD,
                     )
-                if j == 3:
-                    nc.sync.dma_start(out=k_rows(out_1), in_=hn[:])
+                    nc.gpsimd.tensor_tensor(out=hn[:, c0 : c0 + HALF], in0=hn[:, c0 : c0 + HALF], in1=outer[:], op=ADD)
+            if t == 19:
+                nc.sync.dma_start(out=k_rows(out_1), in_=hn[:])
             if g < NG - 1:
                 if i == GROUP - 1:
                     nc.sync.dma_start(out=out_v[:, (t - 3) * N : (t + 1) * N], in_=st[:])

@@ -19,6 +19,9 @@ HALF = 512
 GROUP = 4
 NG = NT // GROUP
 FLOPS = 2 * B * K * N
+IN0 = NT * N // 2 + HALF
+IO_COLS = NT * N + HALF
+STORE_ENDS = [8, 14, 22, 28, 32]
 
 
 def tile_plasticlayer_t_kernel(tc, inp, yin, hebb, w, alpha, eta, out_0, out_1):
@@ -27,9 +30,8 @@ def tile_plasticlayer_t_kernel(tc, inp, yin, hebb, w, alpha, eta, out_0, out_1):
         const = ctx.enter_context(tc.tile_pool(name="const", bufs=1))
         wpool = ctx.enter_context(tc.tile_pool(name="wpool", bufs=1))
         ypool = ctx.enter_context(tc.tile_pool(name="ypool", bufs=1))
-        ipool = ctx.enter_context(tc.tile_pool(name="ipool", bufs=1))
+        iopool = ctx.enter_context(tc.tile_pool(name="iopool", bufs=1))
         gpool = ctx.enter_context(tc.tile_pool(name="gpool", bufs=3))
-        spool = ctx.enter_context(tc.tile_pool(name="spool", bufs=4))
         xpool = ctx.enter_context(tc.psum_pool(name="xpool", bufs=2))
         apool = ctx.enter_context(tc.psum_pool(name="apool", bufs=6))
         ctx.enter_context(tc.manual_schedule())
@@ -47,16 +49,19 @@ def tile_plasticlayer_t_kernel(tc, inp, yin, hebb, w, alpha, eta, out_0, out_1):
         nc.vector.memset(sel[:], 0.0)
         nc.vector.memset(sel[0:1, :], 1.0)
 
-        wt = {}
+        io = iopool.tile([P, IO_COLS], F32, name="io")
+        hebb_t = wpool.tile([P, 4 * N], BF16, name="hebb_t")
+        wt = {
+            "alpha": io[:, 4 * N : 6 * N].bitcast(BF16),
+            "hebb": hebb_t[:],
+            "w": io[:, 6 * N : 8 * N].bitcast(BF16),
+        }
         for nm, src in (("alpha", alpha), ("hebb", hebb), ("w", w)):
-            t_ = wpool.tile([P, 4 * N], BF16, name=nm)
-            nc.sync.dma_start(out=t_[:], in_=k_rows(src))
-            wt[nm] = t_
+            nc.sync.dma_start(out=wt[nm], in_=k_rows(src))
             if nm == "alpha":
                 nc.sync.dma_start(out=eta_row[0:1, 0:1], in_=eta.rearrange("(o x) -> o x", o=1))
 
         yloc = {}
-        iloc = {}
 
         def load_y(t0, n_tiles):
             t_ = ypool.tile([P, n_tiles * K], BF16, name="y%d" % t0)
@@ -65,14 +70,13 @@ def tile_plasticlayer_t_kernel(tc, inp, yin, hebb, w, alpha, eta, out_0, out_1):
                 yloc[t0 + j] = (t_, j * (K // 2))
 
         def load_i(t0, n_tiles):
-            t_ = ipool.tile([P, n_tiles * N], BF16, name="i%d" % t0)
-            nc.sync.dma_start(out=t_[:], in_=inp_v[:, t0 * N : (t0 + n_tiles) * N])
-            for j in range(n_tiles):
-                iloc[t0 + j] = (t_, j * N)
+            nc.sync.dma_start(
+                out=io[:, IN0 + t0 * (N // 2) : IN0 + (t0 + n_tiles) * (N // 2)].bitcast(BF16),
+                in_=inp_v[:, t0 * N : (t0 + n_tiles) * N],
+            )
 
-        load_y(0, 8)
+        load_y(0, 16)
         load_i(0, 8)
-        load_y(8, 8)
         load_i(8, 8)
         load_y(16, 16)
         load_i(16, 16)
@@ -95,9 +99,9 @@ def tile_plasticlayer_t_kernel(tc, inp, yin, hebb, w, alpha, eta, out_0, out_1):
         nc.scalar.copy(out=eta_f[:], in_=eta_ps[:, 0:1])
         nc.scalar.activation(out=om[:], in_=eta_ps[:, 0:1], func=ACT.Copy, bias=1.0, scale=-1.0)
         hn = wpool.tile([P, 4 * N], F32, name="hn")
-        nc.scalar.activation(out=hn[:], in_=wt["hebb"][:], func=ACT.Copy, scale=om[:, 0:1])
-        tmp_all = spool.tile([P, 4 * N], F32, name="tmp_all", tag="st")
-        nc.vector.tensor_tensor(out=tmp_all[:], in0=wt["alpha"][:], in1=wt["hebb"][:], op=MULT)
+        nc.scalar.activation(out=hn[:], in_=wt["hebb"], func=ACT.Copy, scale=om[:, 0:1])
+        tmp_all = io[:, 8 * N : 12 * N]
+        nc.vector.tensor_tensor(out=tmp_all, in0=wt["alpha"], in1=wt["hebb"], op=MULT)
         for u in range(2):
             cols = slice(u * 2 * N, (u + 1) * 2 * N)
             nc.vector.tensor_tensor(
@@ -151,19 +155,14 @@ def tile_plasticlayer_t_kernel(tc, inp, yin, hebb, w, alpha, eta, out_0, out_1):
         banks = transposes(1)
         grouped = regroup(banks)
 
-        st = None
-        st0 = None
         ybs = wpool.tile([P, N], F32, name="ybs")
         ycodes, yscales = q_next
         for t in range(NT):
             g, i = divmod(t, GROUP)
             if i == 0:
                 ycodes, yscales = q_next
-                st = spool.tile([P, GROUP * N], F32, name="st")
-                if g == 0:
-                    st0 = st
-            base = i * N
-            itile, ioff = iloc[t]
+            base = t * N
+            ibase = IN0 + t * (N // 2)
             for h in range(2):
                 acc = apool.tile([P, HALF], F32, name="acc")
                 nc.tensor.matmul_mx(
@@ -176,9 +175,9 @@ def tile_plasticlayer_t_kernel(tc, inp, yin, hebb, w, alpha, eta, out_0, out_1):
                     stop=True,
                 )
                 nc.vector.tensor_tensor(
-                    out=st[:, base + h * HALF : base + (h + 1) * HALF],
+                    out=io[:, base + h * HALF : base + (h + 1) * HALF],
                     in0=acc[:],
-                    in1=itile[:, ioff + h * HALF : ioff + (h + 1) * HALF],
+                    in1=io[:, ibase + h * (HALF // 2) : ibase + (h + 1) * (HALF // 2)].bitcast(BF16),
                     op=ADD,
                 )
             if i == 0 and g + 1 < NG:
@@ -187,14 +186,14 @@ def tile_plasticlayer_t_kernel(tc, inp, yin, hebb, w, alpha, eta, out_0, out_1):
                 banks = transposes(g + 2)
             if i == 2 and g + 2 < NG:
                 grouped = regroup(banks)
-            nc.scalar.activation(out=st[:, base : base + N], in_=st[:, base : base + N], func=ACT.Tanh)
+            nc.scalar.activation(out=io[:, base : base + N], in_=io[:, base : base + N], func=ACT.Tanh)
             if t in (3, 4):
                 h = t - 3
                 yb_h = apool.tile([P, HALF], F32, name="yb%d" % h, tag="acc")
                 nc.tensor.matmul(
                     out=yb_h[:],
                     lhsT=ident[:, 0:1].to_broadcast([P, P]),
-                    rhs=st0[:, h * HALF : (h + 1) * HALF],
+                    rhs=io[:, h * HALF : (h + 1) * HALF],
                     start=True,
                     stop=True,
                 )
@@ -211,10 +210,8 @@ def tile_plasticlayer_t_kernel(tc, inp, yin, hebb, w, alpha, eta, out_0, out_1):
                         op1=ADD,
                     )
                     nc.gpsimd.tensor_tensor(out=hn[:, c0 : c0 + HALF], in0=hn[:, c0 : c0 + HALF], in1=outer[:], op=ADD)
-            if t == 19:
+            if t + 1 in STORE_ENDS:
+                t0 = STORE_ENDS[STORE_ENDS.index(t + 1) - 1] if STORE_ENDS.index(t + 1) > 0 else 0
+                nc.sync.dma_start(out=out_v[:, t0 * N : (t + 1) * N], in_=io[:, t0 * N : (t + 1) * N])
+            if t == 13:
                 nc.sync.dma_start(out=k_rows(out_1), in_=hn[:])
-            if g < NG - 1:
-                if i == GROUP - 1:
-                    nc.sync.dma_start(out=out_v[:, (t - 3) * N : (t + 1) * N], in_=st[:])
-            elif i % 2 == 1:
-                nc.sync.dma_start(out=out_v[:, (t - 1) * N : (t + 1) * N], in_=st[:, (i - 1) * N : (i + 1) * N])

@@ -21,7 +21,7 @@ NG = NT // GROUP
 FLOPS = 2 * B * K * N
 IN0 = NT * N // 2 + HALF
 IO_COLS = NT * N + HALF
-STORE_ENDS = [8, 14, 22, 28, 32]
+STORE_ENDS = [4, 8, 14, 22, 28, 32]
 
 
 def tile_plasticlayer_t_kernel(tc, inp, yin, hebb, w, alpha, eta, out_0, out_1):

@@ -21,6 +21,7 @@ NG = NT // GROUP
 FLOPS = 2 * B * K * N
 IN0 = NT * N // 2 + HALF
 IO_COLS = NT * N + HALF
+DMA_ALIGN = 256
 STORE_ENDS = [4, 8, 14, 22, 28, 32]
 
 
@@ -49,8 +50,8 @@ def tile_plasticlayer_t_kernel(tc, inp, yin, hebb, w, alpha, eta, out_0, out_1):
         nc.vector.memset(sel[:], 0.0)
         nc.vector.memset(sel[0:1, :], 1.0)
 
-        io = iopool.tile([P, IO_COLS], F32, name="io")
-        hebb_t = wpool.tile([P, 4 * N], BF16, name="hebb_t")
+        io = iopool.tile([P, IO_COLS], F32, name="io", align_bytes=DMA_ALIGN)
+        hebb_t = wpool.tile([P, 4 * N], BF16, name="hebb_t", align_bytes=DMA_ALIGN)
         wt = {
             "alpha": io[:, 4 * N : 6 * N].bitcast(BF16),
             "hebb": hebb_t[:],
@@ -64,7 +65,7 @@ def tile_plasticlayer_t_kernel(tc, inp, yin, hebb, w, alpha, eta, out_0, out_1):
         yloc = {}
 
         def load_y(t0, n_tiles):
-            t_ = ypool.tile([P, n_tiles * K], BF16, name="y%d" % t0)
+            t_ = ypool.tile([P, n_tiles * K], BF16, name="y%d" % t0, align_bytes=DMA_ALIGN)
             nc.sync.dma_start(out=t_[:], in_=yin_v[:, t0 * K : (t0 + n_tiles) * K])
             for j in range(n_tiles):
                 yloc[t0 + j] = (t_, j * (K // 2))
@@ -98,7 +99,7 @@ def tile_plasticlayer_t_kernel(tc, inp, yin, hebb, w, alpha, eta, out_0, out_1):
         wscales = wpool.tile([P, N], U8, name="wscales", align_bytes=64)
         nc.scalar.copy(out=eta_f[:], in_=eta_ps[:, 0:1])
         nc.scalar.activation(out=om[:], in_=eta_ps[:, 0:1], func=ACT.Copy, bias=1.0, scale=-1.0)
-        hn = wpool.tile([P, 4 * N], F32, name="hn")
+        hn = wpool.tile([P, 4 * N], F32, name="hn", align_bytes=DMA_ALIGN)
         nc.scalar.activation(out=hn[:], in_=wt["hebb"], func=ACT.Copy, scale=om[:, 0:1])
         tmp_all = io[:, 8 * N : 12 * N]
         nc.vector.tensor_tensor(out=tmp_all, in0=wt["alpha"], in1=wt["hebb"], op=MULT)

from contextlib import ExitStack

import concourse.mybir as mybir
from concourse.masks import make_identity

F32 = mybir.dt.float32
BF16 = mybir.dt.bfloat16
U32 = mybir.dt.uint32
U8 = mybir.dt.uint8
FP8X4 = mybir.dt.float8_e4m3fn_x4
ADD = mybir.AluOpType.add
MULT = mybir.AluOpType.mult
ACT = mybir.ActivationFunctionType

P = 128
B, K, N = 4096, 512, 1024
NT = B // P
HALF = 512
GROUP = 4
NG = NT // GROUP
FLOPS = 2 * B * K * N
IN0 = NT * N // 2 + HALF
IO_COLS = NT * N + HALF
DMA_ALIGN = 256
STORE_ENDS = [4, 8, 14, 22, 28, 32]


def tile_plasticlayer_t_kernel(tc, inp, yin, hebb, w, alpha, eta, out_0, out_1):
    nc = tc.nc
    with ExitStack() as ctx:
        const = ctx.enter_context(tc.tile_pool(name="const", bufs=1))
        wpool = ctx.enter_context(tc.tile_pool(name="wpool", bufs=1))
        ypool = ctx.enter_context(tc.tile_pool(name="ypool", bufs=1))
        iopool = ctx.enter_context(tc.tile_pool(name="iopool", bufs=1))
        gpool = ctx.enter_context(tc.tile_pool(name="gpool", bufs=3))
        xpool = ctx.enter_context(tc.psum_pool(name="xpool", bufs=2))
        apool = ctx.enter_context(tc.psum_pool(name="apool", bufs=6))
        ctx.enter_context(tc.manual_schedule())

        yin_v = yin.rearrange("(p t) k -> p (t k)", t=NT)
        inp_v = inp.rearrange("(p t) n -> p (t n)", t=NT)
        out_v = out_0.rearrange("(p t) n -> p (t n)", t=NT)

        def k_rows(x):
            return x.rearrange("(p j) n -> p (j n)", j=4)

        eta_row = const.tile([P, 32], BF16, name="eta_row")
        nc.vector.memset(eta_row[:], 0.0)
        sel = const.tile([P, P], BF16, name="sel")
        nc.vector.memset(sel[:], 0.0)
        nc.vector.memset(sel[0:1, :], 1.0)

        io = iopool.tile([P, IO_COLS], F32, name="io", align_bytes=DMA_ALIGN)
        hebb_t = wpool.tile([P, 4 * N], BF16, name="hebb_t", align_bytes=DMA_ALIGN)
        wt = {
            "alpha": io[:, 4 * N : 6 * N].bitcast(BF16),
            "hebb": hebb_t[:],
            "w": io[:, 6 * N : 8 * N].bitcast(BF16),
        }
        for nm, src in (("alpha", alpha), ("hebb", hebb), ("w", w)):
            nc.sync.dma_start(out=wt[nm], in_=k_rows(src))
            if nm == "alpha":
                nc.sync.dma_start(out=eta_row[0:1, 0:1], in_=eta.rearrange("(o x) -> o x", o=1))

        yloc = {}

        def load_y(t0, n_tiles):
            t_ = ypool.tile([P, n_tiles * K], BF16, name="y%d" % t0, align_bytes=DMA_ALIGN)
            nc.sync.dma_start(out=t_[:], in_=yin_v[:, t0 * K : (t0 + n_tiles) * K])
            for j in range(n_tiles):
                yloc[t0 + j] = (t_, j * (K // 2))

        def load_i(t0, n_tiles):
            nc.sync.dma_start(
                out=io[:, IN0 + t0 * (N // 2) : IN0 + (t0 + n_tiles) * (N // 2)].bitcast(BF16),
                in_=inp_v[:, t0 * N : (t0 + n_tiles) * N],
            )

        load_y(0, 16)
        load_i(0, 8)
        load_i(8, 8)
        load_y(16, 16)
        load_i(16, 16)

        warm = const.tile([P, 1], F32, name="warm")
        warm2 = const.tile([P, 1], F32, name="warm2")
        nc.vector.memset(warm[:], 0.0)
        nc.scalar.activation(out=warm2[:], in_=warm[:], func=ACT.Tanh)
        ident = const.tile([P, P], F32, name="ident")
        make_identity(nc, ident[:])
        eta_f = const.tile([P, 1], F32, name="eta_f")
        om = const.tile([P, 1], F32, name="om")
        eta_ps = apool.tile([P, HALF], F32, name="eta_ps", tag="acc")
        nc.tensor.matmul(out=eta_ps[:, 0:32], lhsT=sel[:], rhs=eta_row[:], start=True, stop=True)

        wg = wpool.tile([P, 4 * N], BF16, name="wg", align_bytes=64)
        wg_v = wg[:].rearrange("p (n u e) -> p u n e", u=2, e=2)
        wcodes = wpool.tile([P, N], U32, name="wcodes", align_bytes=64)
        wscales = wpool.tile([P, N], U8, name="wscales", align_bytes=64)
        nc.scalar.copy(out=eta_f[:], in_=eta_ps[:, 0:1])
        nc.scalar.activation(out=om[:], in_=eta_ps[:, 0:1], func=ACT.Copy, bias=1.0, scale=-1.0)
        hn = wpool.tile([P, 4 * N], F32, name="hn", align_bytes=DMA_ALIGN)
        nc.scalar.activation(out=hn[:], in_=wt["hebb"], func=ACT.Copy, scale=om[:, 0:1])
        tmp_all = io[:, 8 * N : 12 * N]
        nc.vector.tensor_tensor(out=tmp_all, in0=wt["alpha"], in1=wt["hebb"], op=MULT)
        for u in range(2):
            cols = slice(u * 2 * N, (u + 1) * 2 * N)
            nc.vector.tensor_tensor(
                out=wg_v[:, u],
                in0=tmp_all[:, cols].rearrange("p (e n) -> p n e", e=2),
                in1=wt["w"][:, cols].rearrange("p (e n) -> p n e", e=2),
                op=ADD,
            )

        def transposes(g):
            banks = []
            for j in range(2):
                xt = xpool.tile([P, HALF], F32, name="xt")
                for i in range(2):
                    t = GROUP * g + 2 * j + i
                    ytile, c0 = yloc[t]
                    yw = ytile[:].bitcast(F32)
                    for u in range(2):
                        s0 = (2 * i + u) * P
                        nc.tensor.transpose(xt[:, s0 : s0 + P], yw[:, c0 + u : c0 + K // 2 : 2], ident[:])
                banks.append(xt)
            return banks

        def regroup(banks):
            grouped = gpool.tile([P, GROUP * K], BF16, name="grouped", align_bytes=64, bufs=2)
            gw = grouped[:].bitcast(F32)
            for j in range(2):
                nc.scalar.copy(
                    out=gw[:, j * HALF : (j + 1) * HALF].rearrange("p (i b u) -> p i b u", i=2, u=2),
                    in_=banks[j][:].rearrange("p (i u b) -> p i b u", i=2, u=2),
                )
            return grouped

        def quantise(grouped):
            ycodes = gpool.tile([P, GROUP * P], U32, name="ycodes", align_bytes=64)
            yscales = gpool.tile([P, GROUP * P], U8, name="yscales", align_bytes=64)
            nc.vector.quantize_mx(out=ycodes[:].bitcast(FP8X4), scales=yscales[:], in_=grouped[:])
            return ycodes, yscales

        banks = transposes(0)
        grouped = regroup(banks)
        q_next = quantise(grouped)
        s_k = const.tile([P, 4], F32, name="s_k")
        nc.vector.tensor_scalar(out=s_k[:], in0=grouped[:, 0:4], scalar1=eta_f[:, 0:1], scalar2=None, op0=MULT)
        for h in range(2):
            nc.vector.quantize_mx(
                out=wcodes[:, h * HALF : (h + 1) * HALF].bitcast(FP8X4),
                scales=wscales[:, h * HALF : (h + 1) * HALF],
                in_=wg[:, h * 4 * HALF : (h + 1) * 4 * HALF],
            )
        banks = transposes(1)
        grouped = regroup(banks)

        ybs = wpool.tile([P, N], F32, name="ybs")
        ycodes, yscales = q_next
        for t in range(NT):
            g, i = divmod(t, GROUP)
            if i == 0:
                ycodes, yscales = q_next
            base = t * N
            ibase = IN0 + t * (N // 2)
            for h in range(2):
                acc = apool.tile([P, HALF], F32, name="acc")
                nc.tensor.matmul_mx(
                    out=acc[:],
                    lhsT=ycodes[:, i * P : (i + 1) * P].bitcast(FP8X4),
                    lhsT_scale=yscales[:, i * P : (i + 1) * P],
                    rhs=wcodes[:, h * HALF : (h + 1) * HALF].bitcast(FP8X4),
                    rhs_scale=wscales[:, h * HALF : (h + 1) * HALF],
                    start=True,
                    stop=True,
                )
                nc.vector.tensor_tensor(
                    out=io[:, base + h * HALF : base + (h + 1) * HALF],
                    in0=acc[:],
                    in1=io[:, ibase + h * (HALF // 2) : ibase + (h + 1) * (HALF // 2)].bitcast(BF16),
                    op=ADD,
                )
            if i == 0 and g + 1 < NG:
                q_next = quantise(grouped)
            if i == 1 and g + 2 < NG:
                banks = transposes(g + 2)
            if i == 2 and g + 2 < NG:
                grouped = regroup(banks)
            nc.scalar.activation(out=io[:, base : base + N], in_=io[:, base : base + N], func=ACT.Tanh)
            if t in (3, 4):
                h = t - 3
                yb_h = apool.tile([P, HALF], F32, name="yb%d" % h, tag="acc")
                nc.tensor.matmul(
                    out=yb_h[:],
                    lhsT=ident[:, 0:1].to_broadcast([P, P]),
                    rhs=io[:, h * HALF : (h + 1) * HALF],
                    start=True,
                    stop=True,
                )
                nc.scalar.copy(out=ybs[:, h * HALF : (h + 1) * HALF], in_=yb_h[:])
                for j in range(4):
                    c0 = j * N + h * HALF
                    outer = gpool.tile([P, HALF], F32, name="outer", bufs=2)
                    nc.gpsimd.tensor_scalar(
                        out=outer[:],
                        in0=ybs[:, h * HALF : (h + 1) * HALF],
                        scalar1=s_k[:, j : j + 1],
                        scalar2=0.0,
                        op0=MULT,
                        op1=ADD,
                    )
                    nc.gpsimd.tensor_tensor(out=hn[:, c0 : c0 + HALF], in0=hn[:, c0 : c0 + HALF], in1=outer[:], op=ADD)
            if t + 1 in STORE_ENDS:
                t0 = STORE_ENDS[STORE_ENDS.index(t + 1) - 1] if STORE_ENDS.index(t + 1) > 0 else 0
                nc.sync.dma_start(out=out_v[:, t0 * N : (t + 1) * N], in_=io[:, t0 * N : (t + 1) * N])
            if t == 13:
                nc.sync.dma_start(out=k_rows(out_1), in_=hn[:])
